import numpy as np
import ml_dtypes


def mxq(x, axis, fmt="e4m3"):
    dtype, down = {"e4m3": (ml_dtypes.float8_e4m3fn, 7), "e5m2": (ml_dtypes.float8_e5m2, 14)}[fmt]
    v = np.moveaxis(np.asarray(x, np.float32).astype(ml_dtypes.bfloat16).astype(np.float64), axis, -1)
    blocks = v.reshape(v.shape[:-1] + (-1, 32))
    amax = np.abs(blocks).max(-1, keepdims=True)
    byte = np.maximum(np.where(amax > 0, np.frexp(amax)[1] - 1 + 127, 0) - down, 1)
    scale = np.exp2(byte - 127.0)
    codes = (blocks / scale).astype(np.float32).astype(dtype).astype(np.float64)
    return np.moveaxis((codes * scale).reshape(v.shape), -1, axis)


WIDE = False


def mx_kscale(k):
    if not WIDE:
        return np.ones(k)
    levels = np.array([10, -10, 5, -5, 0])
    if k % 512:
        return np.exp2(np.random.permutation(np.resize(levels, k // 32))).repeat(32)
    a = np.empty((k // 512, 16))
    for p in range(k // 512):
        a[p, :8] = np.random.permutation(np.resize(levels, 8))
        for g in range(8):
            far = levels[np.abs(levels - a[p, g]) >= 10]
            a[p, g + 8] = far[np.random.randint(len(far))]
    return np.exp2(a.ravel()).repeat(32)


BF16 = ml_dtypes.bfloat16


def bf(x):
    return np.asarray(x, np.float32).astype(BF16)


def f64(x):
    return np.asarray(x).astype(np.float64)


B, S, I0, I1, I2, I3, I4, O0, O1, O2, O3, O4, R1, R2, R3, R4 = 4, 2048, 4, 4, 2, 2, 16, 2, 2, 2, 2, 8, 16, 512, 1024, 512
IL, OL = I0 * I1 * I2 * I3, O0 * O1 * O2 * O3
IN, OUT = IL * I4, OL * O4


def setup_inputs():
    s = mx_kscale(R4)
    a = mx_kscale(IN)[::I4]
    return {"x": bf(np.random.standard_normal((B, S, IN)) / np.repeat(a, I4)),
            "t3": bf(np.random.standard_normal((IL, OL, R4)) * s * a[:, None, None]),
            "core4": bf(np.random.standard_normal((R4, I4, O4, 1)) / np.sqrt(R4 * IN) / s[:, None, None, None]),
            "bias": bf(np.random.standard_normal(OUT))}


def reference(x, t3, core4, bias):
    p = mxq(f64(t3).reshape(IL * OL, R4), 1, "e4m3") @ mxq(f64(core4).reshape(R4, I4 * O4), 0, "e4m3")
    m = p.reshape(IL, OL, I4, O4, 1).transpose(0, 2, 1, 3, 4).reshape(IN, OUT, 1)[:, :, 0]
    y = (mxq(f64(x).reshape(B * S, IN), 1, "e4m3") @ mxq(m, 0, "e4m3")) + f64(bias)
    return y.reshape(B, S, OUT)

@@ -1,0 +1,244 @@
+from contextlib import ExitStack
+
+import concourse.mybir as mybir
+from concourse.masks import make_identity
+
+F32 = mybir.dt.float32
+BF16 = mybir.dt.bfloat16
+U32 = mybir.dt.uint32
+U8 = mybir.dt.uint8
+FP8X4 = mybir.dt.float8_e4m3fn_x4
+ADD = mybir.AluOpType.add
+
+P = 128
+TOKENS = 8192
+K2 = 1024
+OUT = 128
+SUB = 4
+GROUP = P * SUB
+NG = TOKENS // GROUP
+BANK_DT = F32
+
+FLOPS = 2 * 1024 * 512 * 128 + 2 * TOKENS * K2 * OUT
+
+
+def tile_linear2mpo_pb_t_kernel(tc, x, t3, core4, bias, out):
+    nc = tc.nc
+    x_v = x.flatten_outer_dims().rearrange("(g p n) k -> g p n k", p=P, n=SUB)
+    o_v = out.flatten_outer_dims().rearrange("(g p n) c -> g p n c", p=P, n=SUB)
+    t3_v = t3.rearrange("(h b c) o r -> b (c o) h r", h=2, b=4)
+    c4_v = core4.rearrange("(p j) i o z -> p j (i o z)", j=4)
+    bias_v = bias.rearrange("(a n) -> a n", a=1)
+
+    with ExitStack() as ctx:
+        keep = ctx.enter_context(tc.tile_pool(name="keep", bufs=1))
+        xin = ctx.enter_context(tc.tile_pool(name="xin", bufs=8))
+        work = ctx.enter_context(tc.tile_pool(name="work", bufs=3))
+        ps_t = ctx.enter_context(tc.psum_pool(name="ps_t", bufs=6))
+        ps_a = ctx.enter_context(tc.psum_pool(name="ps_a", bufs=2))
+        ctx.enter_context(tc.manual_schedule())
+
+        brow = keep.tile([P, OUT], BF16, name="brow")
+        ones = keep.tile([P, P], BF16, name="ones")
+        nc.vector.memset(brow[:], 0.0)
+        nc.vector.memset(ones[:], 1.0)
+        ident = keep.tile([P, P], F32, name="ident")
+        make_identity(nc, ident[:])
+
+        c4_sb = keep.tile([P, 4, 128], BF16, name="c4_sb")
+        nc.scalar.dma_start(out=c4_sb[:], in_=c4_v)
+        nc.scalar.dma_start(out=brow[0:1, :], in_=bias_v)
+
+        t3_sb = keep.tile([P, 4, 2, 512], BF16, name="t3_sb")
+        for b in range(4):
+            nc.sync.dma_start(out=t3_sb[:, b], in_=t3_v[b])
+
+        x_tiles = {}
+
+        def load_x(i):
+            x_sb = xin.tile([P, SUB, K2], BF16, name="x_sb")
+            nc.sync.dma_start(out=x_sb[:], in_=x_v[i])
+            x_tiles[i] = x_sb
+
+        for i in range(8):
+            load_x(i)
+
+        bias_t = keep.tile([P, SUB, OUT], F32, name="bias_t")
+
+        c4g = keep.tile([P, 512], BF16, name="c4g", align_bytes=64)
+        nc.vector.tensor_copy(
+            out=c4g[:].rearrange("p (x h j) -> p x h j", x=32, h=4, j=4),
+            in_=c4_sb[:].rearrange("p j (h x) -> p x h j", h=4),
+        )
+        c4c = keep.tile([P, 128], U32, name="c4c", align_bytes=64)
+        c4s = keep.tile([P, 128], U8, name="c4s", align_bytes=64)
+
+        t3w = t3_sb[:].rearrange("p b h r -> p (b h r)").bitcast(F32)
+        t3g = keep.tile([P, 4096], BF16, name="t3g", align_bytes=64)
+        t3gw = t3g[:].bitcast(F32).rearrange("q (j b o s) -> q j b o s", j=8, b=4, o=16, s=4)
+        for b in range(4):
+            tp = ps_t.tile([P, 4, P], F32, name="tp", tag="tp")
+            for h in range(2):
+                for u in range(2):
+                    base = (b * 2 + h) * 256
+                    nc.tensor.transpose(tp[:, 2 * h + u, :], t3w[:, base + u : base + 256 : 2], ident[:])
+            src = tp[:].rearrange("q s (j o) -> q j o s", j=8)
+            if b % 2 == 0:
+                nc.scalar.copy(out=t3gw[:, :, b], in_=src)
+            else:
+                nc.vector.tensor_copy(out=t3gw[:, :, b], in_=src)
+            if b == 0:
+                nc.vector.quantize_mx(out=c4c[:].bitcast(FP8X4), scales=c4s[:], in_=c4g[:])
+            if b == 1:
+                pb = ps_a.tile([P, OUT], F32, name="pb", tag="acc")
+                nc.tensor.matmul(pb[:], lhsT=ones[:], rhs=brow[:], start=True, stop=True)
+                for n in range(SUB):
+                    nc.scalar.copy(out=bias_t[:, n, :], in_=pb[:])
+        t3c = keep.tile([P, 1024], U32, name="t3c", align_bytes=64)
+        t3s = keep.tile([P, 1024], U8, name="t3s", align_bytes=64)
+
+        xg_tiles = {}
+        xc_tiles = {}
+        acc_tiles = {}
+
+        def transposes(i):
+            xw = x_tiles[i][:].rearrange("p n k -> p (n k)").bitcast(F32)
+            xg = work.tile([P, SUB * K2], BF16, name="xg", align_bytes=64)
+            xgw = xg[:].bitcast(F32)
+            for n in range(SUB):
+                tp = ps_t.tile([P, 4, P], F32, name="tp", tag="tp")
+                for g in range(2):
+                    for u in range(2):
+                        base = n * 512 + g * 256
+                        nc.tensor.transpose(tp[:, 2 * g + u, :], xw[:, base + u : base + 256 : 2], ident[:])
+                nc.scalar.copy(
+                    out=xgw[:, n * 512 : (n + 1) * 512].rearrange("q (g t u) -> q g t u", g=2, u=2),
+                    in_=tp[:].rearrange("q (g u) t -> q g t u", g=2),
+                )
+            xg_tiles[i] = xg
+
+        def new_codes(i):
+            xc = work.tile([P, SUB * 256], U32, name="xc", align_bytes=64)
+            xs = work.tile([P, SUB * 256], U8, name="xs", align_bytes=64)
+            xc_tiles[i] = (xc, xs)
+
+        def quant(i, n0, n1):
+            xc, xs = xc_tiles[i]
+            nc.vector.quantize_mx(
+                out=xc[:, n0 * 256 : n1 * 256].bitcast(FP8X4),
+                scales=xs[:, n0 * 256 : n1 * 256],
+                in_=xg_tiles[i][:, n0 * 1024 : n1 * 1024],
+            )
+
+        def mm(i):
+            xc, xs = xc_tiles[i]
+            acc = ps_a.tile([P, SUB, OUT], F32, name="acc", tag="acc")
+            for n in range(SUB):
+                for g in range(2):
+                    cols = slice((n * 2 + g) * 128, (n * 2 + g + 1) * 128)
+                    nc.tensor.matmul_mx(
+                        out=acc[:, n, :],
+                        lhsT=xc[:, cols].bitcast(FP8X4),
+                        lhsT_scale=xs[:, cols],
+                        rhs=mc[:, g * 128 : (g + 1) * 128].bitcast(FP8X4),
+                        rhs_scale=ms[:, g * 128 : (g + 1) * 128],
+                        start=(g == 0),
+                        stop=(g == 1),
+                    )
+            acc_tiles[i] = acc
+
+        def finish(i):
+            y = work.tile([P, SUB, OUT], F32, name="y")
+            nc.vector.tensor_tensor(out=y[:], in0=acc_tiles[i][:], in1=bias_t[:], op=ADD)
+            nc.sync.dma_start(out=o_v[i], in_=y[:])
+
+        for half in range(2):
+            nc.vector.quantize_mx(
+                out=t3c[:, half * 512 : (half + 1) * 512].bitcast(FP8X4),
+                scales=t3s[:, half * 512 : (half + 1) * 512],
+                in_=t3g[:, half * 2048 : (half + 1) * 2048],
+            )
+        transposes(0)
+
+        mA = keep.tile([P, 1024], BF16, name="mA", align_bytes=64)
+        mAv = mA[:].rearrange("m (x j i) -> m x j i", x=32, j=8, i=4)
+        pms = []
+        for hh in range(2):
+            pm = ps_a.tile([P, 4, 128], BANK_DT, name="pm", tag="acc")
+            for jj in range(4):
+                j = hh * 4 + jj
+                nc.tensor.matmul_mx(
+                    out=pm[:, jj, :],
+                    lhsT=t3c[:, j * 128 : (j + 1) * 128].bitcast(FP8X4),
+                    lhsT_scale=t3s[:, j * 128 : (j + 1) * 128],
+                    rhs=c4c[:].bitcast(FP8X4),
+                    rhs_scale=c4s[:],
+                    start=True,
+                    stop=True,
+                )
+            pms.append(pm)
+
+        transposes(1)
+        new_codes(0)
+        mB = keep.tile([P, 1024], BF16, name="mB", align_bytes=64)
+        mG = keep.tile([P, 1024], BF16, name="mG", align_bytes=64)
+        mc = keep.tile([P, 256], U32, name="mc", align_bytes=64)
+        ms = keep.tile([P, 256], U8, name="ms", align_bytes=64)
+        for hh in range(2):
+            nc.vector.tensor_copy(
+                out=mAv[:, :, 4 * hh : 4 * hh + 4, :],
+                in_=pms[hh][:].rearrange("m j (x i) -> m x j i", i=4),
+            )
+        quant(0, 0, 1)
+        nc.vector.transpose(out=mB[:], in_=mA[:])
+        quant(0, 1, 2)
+        mGv = mG[:].rearrange("p (g a o t) -> p g a o t", g=2, a=16, o=8, t=4)
+        mBv = mB[:].rearrange("p (t o a g) -> p g a o t", t=4, o=8, a=16, g=2)
+        for g in range(2):
+            nc.vector.tensor_copy(out=mGv[:, g], in_=mBv[:, g])
+        quant(0, 2, 3)
+        nc.vector.quantize_mx(out=mc[:].bitcast(FP8X4), scales=ms[:], in_=mG[:])
+        quant(0, 3, 4)
+
+        transposes(2)
+        mm(0)
+        new_codes(1)
+        quant(1, 0, 2)
+        quant(1, 2, 4)
+        load_x(8)
+
+        transposes(3)
+        new_codes(2)
+        quant(2, 0, 2)
+        quant(2, 2, 4)
+        mm(1)
+        finish(0)
+        mm(2)
+        finish(1)
+        load_x(9)
+
+        for tick in range(4, NG - 1):
+            transposes(tick)
+            new_codes(tick - 1)
+            quant(tick - 1, 0, 2)
+            quant(tick - 1, 2, 4)
+            mm(tick - 1)
+            finish(tick - 2)
+            if tick + 6 < NG:
+                load_x(tick + 6)
+
+        last = NG - 1
+        transposes(last)
+        new_codes(last - 1)
+        quant(last - 1, 0, 2)
+        quant(last - 1, 2, 4)
+        new_codes(last)
+        quant(last, 0, 1)
+        finish(last - 2)
+        quant(last, 1, 2)
+        quant(last, 2, 3)
+        quant(last, 3, 4)
+        mm(last - 1)
+        mm(last)
+        finish(last - 1)
+        finish(last)

@@ -18,6 +18,8 @@ SUB = 4
 GROUP = P * SUB
 NG = TOKENS // GROUP
 BANK_DT = F32
+PIECES = {0: 4, 1: 2, 2: 2}
+FIRST_PERMUTED = 3
 
 FLOPS = 2 * 1024 * 512 * 128 + 2 * TOKENS * K2 * OUT
 
@@ -32,16 +34,18 @@ def tile_linear2mpo_pb_t_kernel(tc, x, t3, core4, bias, out):
 
     with ExitStack() as ctx:
         keep = ctx.enter_context(tc.tile_pool(name="keep", bufs=1))
-        xin = ctx.enter_context(tc.tile_pool(name="xin", bufs=8))
+        xin = ctx.enter_context(tc.tile_pool(name="xin", bufs=12))
         work = ctx.enter_context(tc.tile_pool(name="work", bufs=3))
+        yout = ctx.enter_context(tc.tile_pool(name="yout", bufs=NG))
         ps_t = ctx.enter_context(tc.psum_pool(name="ps_t", bufs=6))
         ps_a = ctx.enter_context(tc.psum_pool(name="ps_a", bufs=2))
         ctx.enter_context(tc.manual_schedule())
 
         brow = keep.tile([P, OUT], BF16, name="brow")
-        ones = keep.tile([P, P], BF16, name="ones")
+        wide = keep.tile([P, 512], BF16, name="wide")
+        nc.vector.memset(wide[:], 1.0)
         nc.vector.memset(brow[:], 0.0)
-        nc.vector.memset(ones[:], 1.0)
+        ones = wide[:, 0:P]
         ident = keep.tile([P, P], F32, name="ident")
         make_identity(nc, ident[:])
 
@@ -53,25 +57,40 @@ def tile_linear2mpo_pb_t_kernel(tc, x, t3, core4, bias, out):
         for b in range(4):
             nc.sync.dma_start(out=t3_sb[:, b], in_=t3_v[b])
 
-        x_tiles = {}
+        x_words = {}
 
         def load_x(i):
-            x_sb = xin.tile([P, SUB, K2], BF16, name="x_sb")
-            nc.sync.dma_start(out=x_sb[:], in_=x_v[i])
-            x_tiles[i] = x_sb
+            pieces = PIECES.get(i, 1)
+            per = SUB // pieces
+            for c in range(pieces):
+                x_sb = xin.tile([P, per, K2], BF16, name="x_sb")
+                nc.sync.dma_start(out=x_sb[:], in_=x_v[i][:, c * per : (c + 1) * per, :])
+                xw = x_sb[:].rearrange("p n k -> p (n k)").bitcast(F32)
+                for n in range(per):
+                    x_words[(i, c * per + n)] = xw[:, n * 512 : (n + 1) * 512]
+                if pieces == 1:
+                    x_words[(i, "tail")] = xw[:, 1024:2048]
 
-        for i in range(8):
+        for i in range(7):
             load_x(i)
+
+        def dummy(count):
+            wu = ps_t.tile([P, 512], F32, name="wu", tag="tp")
+            for r in range(count):
+                nc.tensor.matmul(wu[:], lhsT=ones, rhs=wide[:], start=True, stop=True)
+
+        dummy(5)
 
         bias_t = keep.tile([P, SUB, OUT], F32, name="bias_t")
 
         c4g = keep.tile([P, 512], BF16, name="c4g", align_bytes=64)
-        nc.vector.tensor_copy(
+        nc.scalar.copy(
             out=c4g[:].rearrange("p (x h j) -> p x h j", x=32, h=4, j=4),
             in_=c4_sb[:].rearrange("p j (h x) -> p x h j", h=4),
         )
         c4c = keep.tile([P, 128], U32, name="c4c", align_bytes=64)
         c4s = keep.tile([P, 128], U8, name="c4s", align_bytes=64)
+        nc.vector.quantize_mx(out=c4c[:].bitcast(FP8X4), scales=c4s[:], in_=c4g[:])
 
         t3w = t3_sb[:].rearrange("p b h r -> p (b h r)").bitcast(F32)
         t3g = keep.tile([P, 4096], BF16, name="t3g", align_bytes=64)
@@ -87,34 +106,48 @@ def tile_linear2mpo_pb_t_kernel(tc, x, t3, core4, bias, out):
                 nc.scalar.copy(out=t3gw[:, :, b], in_=src)
             else:
                 nc.vector.tensor_copy(out=t3gw[:, :, b], in_=src)
-            if b == 0:
-                nc.vector.quantize_mx(out=c4c[:].bitcast(FP8X4), scales=c4s[:], in_=c4g[:])
             if b == 1:
                 pb = ps_a.tile([P, OUT], F32, name="pb", tag="acc")
-                nc.tensor.matmul(pb[:], lhsT=ones[:], rhs=brow[:], start=True, stop=True)
+                nc.tensor.matmul(pb[:], lhsT=ones, rhs=brow[:], start=True, stop=True)
                 for n in range(SUB):
                     nc.scalar.copy(out=bias_t[:, n, :], in_=pb[:])
+            if b % 2 == 1:
+                dummy(1)
         t3c = keep.tile([P, 1024], U32, name="t3c", align_bytes=64)
         t3s = keep.tile([P, 1024], U8, name="t3s", align_bytes=64)
 
+        xp_tiles = {}
         xg_tiles = {}
         xc_tiles = {}
         acc_tiles = {}
 
-        def transposes(i):
-            xw = x_tiles[i][:].rearrange("p n k -> p (n k)").bitcast(F32)
+        def permute(i):
+            xp = work.tile([P, 1024], F32, name="xp")
+            nc.vector.tensor_copy(
+                out=xp[:].rearrange("p (a u q) -> p a u q", a=4, u=2),
+                in_=x_words[(i, "tail")].rearrange("p (a q u) -> p a u q", a=4, u=2),
+            )
+            xp_tiles[i] = xp
+
+        def transposes(i, mid_dummy):
             xg = work.tile([P, SUB * K2], BF16, name="xg", align_bytes=64)
             xgw = xg[:].bitcast(F32)
             for n in range(SUB):
                 tp = ps_t.tile([P, 4, P], F32, name="tp", tag="tp")
                 for g in range(2):
                     for u in range(2):
-                        base = n * 512 + g * 256
-                        nc.tensor.transpose(tp[:, 2 * g + u, :], xw[:, base + u : base + 256 : 2], ident[:])
+                        if i >= FIRST_PERMUTED and n >= 2:
+                            base = ((n - 2) * 4 + g * 2 + u) * P
+                            src = xp_tiles[i][:, base : base + P]
+                        else:
+                            src = x_words[(i, n)][:, g * 256 + u : (g + 1) * 256 : 2]
+                        nc.tensor.transpose(tp[:, 2 * g + u, :], src, ident[:])
                 nc.scalar.copy(
                     out=xgw[:, n * 512 : (n + 1) * 512].rearrange("q (g t u) -> q g t u", g=2, u=2),
                     in_=tp[:].rearrange("q (g u) t -> q g t u", g=2),
                 )
+                if mid_dummy and n == 1:
+                    dummy(1)
             xg_tiles[i] = xg
 
         def new_codes(i):
@@ -148,7 +181,7 @@ def tile_linear2mpo_pb_t_kernel(tc, x, t3, core4, bias, out):
             acc_tiles[i] = acc
 
         def finish(i):
-            y = work.tile([P, SUB, OUT], F32, name="y")
+            y = yout.tile([P, SUB, OUT], F32, name="y")
             nc.vector.tensor_tensor(out=y[:], in0=acc_tiles[i][:], in1=bias_t[:], op=ADD)
             nc.sync.dma_start(out=o_v[i], in_=y[:])
 
@@ -158,7 +191,9 @@ def tile_linear2mpo_pb_t_kernel(tc, x, t3, core4, bias, out):
                 scales=t3s[:, half * 512 : (half + 1) * 512],
                 in_=t3g[:, half * 2048 : (half + 1) * 2048],
             )
-        transposes(0)
+        transposes(0, True)
+        for i in range(7, 11):
+            load_x(i)
 
         mA = keep.tile([P, 1024], BF16, name="mA", align_bytes=64)
         mAv = mA[:].rearrange("m (x j i) -> m x j i", x=32, j=8, i=4)
@@ -177,37 +212,38 @@ def tile_linear2mpo_pb_t_kernel(tc, x, t3, core4, bias, out):
                     stop=True,
                 )
             pms.append(pm)
-
-        transposes(1)
         new_codes(0)
+        for n in range(SUB):
+            quant(0, n, n + 1)
+        nc.scalar.copy(out=mAv[:, :, 0:4, :], in_=pms[0][:].rearrange("m j (x i) -> m x j i", i=4))
+        nc.vector.tensor_copy(out=mAv[:, :, 4:8, :], in_=pms[1][:].rearrange("m j (x i) -> m x j i", i=4))
+
+        transposes(1, True)
+        dummy(1)
+        for i in range(11, 13):
+            load_x(i)
         mB = keep.tile([P, 1024], BF16, name="mB", align_bytes=64)
         mG = keep.tile([P, 1024], BF16, name="mG", align_bytes=64)
         mc = keep.tile([P, 256], U32, name="mc", align_bytes=64)
         ms = keep.tile([P, 256], U8, name="ms", align_bytes=64)
-        for hh in range(2):
-            nc.vector.tensor_copy(
-                out=mAv[:, :, 4 * hh : 4 * hh + 4, :],
-                in_=pms[hh][:].rearrange("m j (x i) -> m x j i", i=4),
-            )
-        quant(0, 0, 1)
         nc.vector.transpose(out=mB[:], in_=mA[:])
-        quant(0, 1, 2)
         mGv = mG[:].rearrange("p (g a o t) -> p g a o t", g=2, a=16, o=8, t=4)
         mBv = mB[:].rearrange("p (t o a g) -> p g a o t", t=4, o=8, a=16, g=2)
         for g in range(2):
             nc.vector.tensor_copy(out=mGv[:, g], in_=mBv[:, g])
-        quant(0, 2, 3)
         nc.vector.quantize_mx(out=mc[:].bitcast(FP8X4), scales=ms[:], in_=mG[:])
-        quant(0, 3, 4)
 
-        transposes(2)
+        transposes(2, False)
+        for i in range(13, 15):
+            load_x(i)
         mm(0)
         new_codes(1)
         quant(1, 0, 2)
         quant(1, 2, 4)
-        load_x(8)
+        permute(3)
 
-        transposes(3)
+        transposes(3, False)
+        load_x(15)
         new_codes(2)
         quant(2, 0, 2)
         quant(2, 2, 4)
@@ -215,20 +251,19 @@ def tile_linear2mpo_pb_t_kernel(tc, x, t3, core4, bias, out):
         finish(0)
         mm(2)
         finish(1)
-        load_x(9)
+        permute(4)
 
         for tick in range(4, NG - 1):
-            transposes(tick)
+            transposes(tick, False)
             new_codes(tick - 1)
             quant(tick - 1, 0, 2)
             quant(tick - 1, 2, 4)
             mm(tick - 1)
             finish(tick - 2)
-            if tick + 6 < NG:
-                load_x(tick + 6)
+            permute(tick + 1)
 
         last = NG - 1
-        transposes(last)
+        transposes(last, False)
         new_codes(last - 1)
         quant(last - 1, 0, 2)
         quant(last - 1, 2, 4)

@@ -74,13 +74,6 @@ def tile_linear2mpo_pb_t_kernel(tc, x, t3, core4, bias, out):
         for i in range(7):
             load_x(i)
 
-        def dummy(count):
-            wu = ps_t.tile([P, 512], F32, name="wu", tag="tp")
-            for r in range(count):
-                nc.tensor.matmul(wu[:], lhsT=ones, rhs=wide[:], start=True, stop=True)
-
-        dummy(5)
-
         bias_t = keep.tile([P, SUB, OUT], F32, name="bias_t")
 
         c4g = keep.tile([P, 512], BF16, name="c4g", align_bytes=64)
@@ -111,8 +104,6 @@ def tile_linear2mpo_pb_t_kernel(tc, x, t3, core4, bias, out):
                 nc.tensor.matmul(pb[:], lhsT=ones, rhs=brow[:], start=True, stop=True)
                 for n in range(SUB):
                     nc.scalar.copy(out=bias_t[:, n, :], in_=pb[:])
-            if b % 2 == 1:
-                dummy(1)
         t3c = keep.tile([P, 1024], U32, name="t3c", align_bytes=64)
         t3s = keep.tile([P, 1024], U8, name="t3s", align_bytes=64)
 
@@ -146,8 +137,6 @@ def tile_linear2mpo_pb_t_kernel(tc, x, t3, core4, bias, out):
                     out=xgw[:, n * 512 : (n + 1) * 512].rearrange("q (g t u) -> q g t u", g=2, u=2),
                     in_=tp[:].rearrange("q (g u) t -> q g t u", g=2),
                 )
-                if mid_dummy and n == 1:
-                    dummy(1)
             xg_tiles[i] = xg
 
         def new_codes(i):
@@ -219,7 +208,6 @@ def tile_linear2mpo_pb_t_kernel(tc, x, t3, core4, bias, out):
         nc.vector.tensor_copy(out=mAv[:, :, 4:8, :], in_=pms[1][:].rearrange("m j (x i) -> m x j i", i=4))
 
         transposes(1, True)
-        dummy(1)
         for i in range(11, 13):
             load_x(i)
         mB = keep.tile([P, 1024], BF16, name="mB", align_bytes=64)

from contextlib import ExitStack

import concourse.mybir as mybir
from concourse.masks import make_identity

F32 = mybir.dt.float32
BF16 = mybir.dt.bfloat16
U32 = mybir.dt.uint32
U8 = mybir.dt.uint8
FP8X4 = mybir.dt.float8_e4m3fn_x4
ADD = mybir.AluOpType.add

P = 128
TOKENS = 8192
K2 = 1024
OUT = 128
SUB = 4
GROUP = P * SUB
NG = TOKENS // GROUP
BANK_DT = F32
PIECES = {0: 4, 1: 2, 2: 2}
FIRST_PERMUTED = 3

FLOPS = 2 * 1024 * 512 * 128 + 2 * TOKENS * K2 * OUT


def tile_linear2mpo_pb_t_kernel(tc, x, t3, core4, bias, out):
    nc = tc.nc
    x_v = x.flatten_outer_dims().rearrange("(g p n) k -> g p n k", p=P, n=SUB)
    o_v = out.flatten_outer_dims().rearrange("(g p n) c -> g p n c", p=P, n=SUB)
    t3_v = t3.rearrange("(h b c) o r -> b (c o) h r", h=2, b=4)
    c4_v = core4.rearrange("(p j) i o z -> p j (i o z)", j=4)
    bias_v = bias.rearrange("(a n) -> a n", a=1)

    with ExitStack() as ctx:
        keep = ctx.enter_context(tc.tile_pool(name="keep", bufs=1))
        xin = ctx.enter_context(tc.tile_pool(name="xin", bufs=12))
        work = ctx.enter_context(tc.tile_pool(name="work", bufs=3))
        yout = ctx.enter_context(tc.tile_pool(name="yout", bufs=NG))
        ps_t = ctx.enter_context(tc.psum_pool(name="ps_t", bufs=6))
        ps_a = ctx.enter_context(tc.psum_pool(name="ps_a", bufs=2))
        ctx.enter_context(tc.manual_schedule())

        brow = keep.tile([P, OUT], BF16, name="brow")
        wide = keep.tile([P, 512], BF16, name="wide")
        nc.vector.memset(wide[:], 1.0)
        nc.vector.memset(brow[:], 0.0)
        ones = wide[:, 0:P]
        ident = keep.tile([P, P], F32, name="ident")
        make_identity(nc, ident[:])

        c4_sb = keep.tile([P, 4, 128], BF16, name="c4_sb")
        nc.scalar.dma_start(out=c4_sb[:], in_=c4_v)
        nc.scalar.dma_start(out=brow[0:1, :], in_=bias_v)

        t3_sb = keep.tile([P, 4, 2, 512], BF16, name="t3_sb")
        for b in range(4):
            nc.sync.dma_start(out=t3_sb[:, b], in_=t3_v[b])

        x_words = {}

        def load_x(i):
            pieces = PIECES.get(i, 1)
            per = SUB // pieces
            for c in range(pieces):
                x_sb = xin.tile([P, per, K2], BF16, name="x_sb")
                nc.sync.dma_start(out=x_sb[:], in_=x_v[i][:, c * per : (c + 1) * per, :])
                xw = x_sb[:].rearrange("p n k -> p (n k)").bitcast(F32)
                for n in range(per):
                    x_words[(i, c * per + n)] = xw[:, n * 512 : (n + 1) * 512]
                if pieces == 1:
                    x_words[(i, "tail")] = xw[:, 1024:2048]

        for i in range(7):
            load_x(i)

        bias_t = keep.tile([P, SUB, OUT], F32, name="bias_t")

        c4g = keep.tile([P, 512], BF16, name="c4g", align_bytes=64)
        nc.scalar.copy(
            out=c4g[:].rearrange("p (x h j) -> p x h j", x=32, h=4, j=4),
            in_=c4_sb[:].rearrange("p j (h x) -> p x h j", h=4),
        )
        c4c = keep.tile([P, 128], U32, name="c4c", align_bytes=64)
        c4s = keep.tile([P, 128], U8, name="c4s", align_bytes=64)
        nc.vector.quantize_mx(out=c4c[:].bitcast(FP8X4), scales=c4s[:], in_=c4g[:])

        t3w = t3_sb[:].rearrange("p b h r -> p (b h r)").bitcast(F32)
        t3g = keep.tile([P, 4096], BF16, name="t3g", align_bytes=64)
        t3gw = t3g[:].bitcast(F32).rearrange("q (j b o s) -> q j b o s", j=8, b=4, o=16, s=4)
        for b in range(4):
            tp = ps_t.tile([P, 4, P], F32, name="tp", tag="tp")
            for h in range(2):
                for u in range(2):
                    base = (b * 2 + h) * 256
                    nc.tensor.transpose(tp[:, 2 * h + u, :], t3w[:, base + u : base + 256 : 2], ident[:])
            src = tp[:].rearrange("q s (j o) -> q j o s", j=8)
            if b % 2 == 0:
                nc.scalar.copy(out=t3gw[:, :, b], in_=src)
            else:
                nc.vector.tensor_copy(out=t3gw[:, :, b], in_=src)
            if b == 1:
                pb = ps_a.tile([P, OUT], F32, name="pb", tag="acc")
                nc.tensor.matmul(pb[:], lhsT=ones, rhs=brow[:], start=True, stop=True)
                for n in range(SUB):
                    nc.scalar.copy(out=bias_t[:, n, :], in_=pb[:])
        t3c = keep.tile([P, 1024], U32, name="t3c", align_bytes=64)
        t3s = keep.tile([P, 1024], U8, name="t3s", align_bytes=64)

        xp_tiles = {}
        xg_tiles = {}
        xc_tiles = {}
        acc_tiles = {}

        def permute(i):
            xp = work.tile([P, 1024], F32, name="xp")
            nc.vector.tensor_copy(
                out=xp[:].rearrange("p (a u q) -> p a u q", a=4, u=2),
                in_=x_words[(i, "tail")].rearrange("p (a q u) -> p a u q", a=4, u=2),
            )
            xp_tiles[i] = xp

        def transposes(i, mid_dummy):
            xg = work.tile([P, SUB * K2], BF16, name="xg", align_bytes=64)
            xgw = xg[:].bitcast(F32)
            for n in range(SUB):
                tp = ps_t.tile([P, 4, P], F32, name="tp", tag="tp")
                for g in range(2):
                    for u in range(2):
                        if i >= FIRST_PERMUTED and n >= 2:
                            base = ((n - 2) * 4 + g * 2 + u) * P
                            src = xp_tiles[i][:, base : base + P]
                        else:
                            src = x_words[(i, n)][:, g * 256 + u : (g + 1) * 256 : 2]
                        nc.tensor.transpose(tp[:, 2 * g + u, :], src, ident[:])
                nc.scalar.copy(
                    out=xgw[:, n * 512 : (n + 1) * 512].rearrange("q (g t u) -> q g t u", g=2, u=2),
                    in_=tp[:].rearrange("q (g u) t -> q g t u", g=2),
                )
            xg_tiles[i] = xg

        def new_codes(i):
            xc = work.tile([P, SUB * 256], U32, name="xc", align_bytes=64)
            xs = work.tile([P, SUB * 256], U8, name="xs", align_bytes=64)
            xc_tiles[i] = (xc, xs)

        def quant(i, n0, n1):
            xc, xs = xc_tiles[i]
            nc.vector.quantize_mx(
                out=xc[:, n0 * 256 : n1 * 256].bitcast(FP8X4),
                scales=xs[:, n0 * 256 : n1 * 256],
                in_=xg_tiles[i][:, n0 * 1024 : n1 * 1024],
            )

        def mm(i):
            xc, xs = xc_tiles[i]
            acc = ps_a.tile([P, SUB, OUT], F32, name="acc", tag="acc")
            for n in range(SUB):
                for g in range(2):
                    cols = slice((n * 2 + g) * 128, (n * 2 + g + 1) * 128)
                    nc.tensor.matmul_mx(
                        out=acc[:, n, :],
                        lhsT=xc[:, cols].bitcast(FP8X4),
                        lhsT_scale=xs[:, cols],
                        rhs=mc[:, g * 128 : (g + 1) * 128].bitcast(FP8X4),
                        rhs_scale=ms[:, g * 128 : (g + 1) * 128],
                        start=(g == 0),
                        stop=(g == 1),
                    )
            acc_tiles[i] = acc

        def finish(i):
            y = yout.tile([P, SUB, OUT], F32, name="y")
            nc.vector.tensor_tensor(out=y[:], in0=acc_tiles[i][:], in1=bias_t[:], op=ADD)
            nc.sync.dma_start(out=o_v[i], in_=y[:])

        for half in range(2):
            nc.vector.quantize_mx(
                out=t3c[:, half * 512 : (half + 1) * 512].bitcast(FP8X4),
                scales=t3s[:, half * 512 : (half + 1) * 512],
                in_=t3g[:, half * 2048 : (half + 1) * 2048],
            )
        transposes(0, True)
        for i in range(7, 11):
            load_x(i)

        mA = keep.tile([P, 1024], BF16, name="mA", align_bytes=64)
        mAv = mA[:].rearrange("m (x j i) -> m x j i", x=32, j=8, i=4)
        pms = []
        for hh in range(2):
            pm = ps_a.tile([P, 4, 128], BANK_DT, name="pm", tag="acc")
            for jj in range(4):
                j = hh * 4 + jj
                nc.tensor.matmul_mx(
                    out=pm[:, jj, :],
                    lhsT=t3c[:, j * 128 : (j + 1) * 128].bitcast(FP8X4),
                    lhsT_scale=t3s[:, j * 128 : (j + 1) * 128],
                    rhs=c4c[:].bitcast(FP8X4),
                    rhs_scale=c4s[:],
                    start=True,
                    stop=True,
                )
            pms.append(pm)
        new_codes(0)
        for n in range(SUB):
            quant(0, n, n + 1)
        nc.scalar.copy(out=mAv[:, :, 0:4, :], in_=pms[0][:].rearrange("m j (x i) -> m x j i", i=4))
        nc.vector.tensor_copy(out=mAv[:, :, 4:8, :], in_=pms[1][:].rearrange("m j (x i) -> m x j i", i=4))

        transposes(1, True)
        for i in range(11, 13):
            load_x(i)
        mB = keep.tile([P, 1024], BF16, name="mB", align_bytes=64)
        mG = keep.tile([P, 1024], BF16, name="mG", align_bytes=64)
        mc = keep.tile([P, 256], U32, name="mc", align_bytes=64)
        ms = keep.tile([P, 256], U8, name="ms", align_bytes=64)
        nc.vector.transpose(out=mB[:], in_=mA[:])
        mGv = mG[:].rearrange("p (g a o t) -> p g a o t", g=2, a=16, o=8, t=4)
        mBv = mB[:].rearrange("p (t o a g) -> p g a o t", t=4, o=8, a=16, g=2)
        for g in range(2):
            nc.vector.tensor_copy(out=mGv[:, g], in_=mBv[:, g])
        nc.vector.quantize_mx(out=mc[:].bitcast(FP8X4), scales=ms[:], in_=mG[:])

        transposes(2, False)
        for i in range(13, 15):
            load_x(i)
        mm(0)
        new_codes(1)
        quant(1, 0, 2)
        quant(1, 2, 4)
        permute(3)

        transposes(3, False)
        load_x(15)
        new_codes(2)
        quant(2, 0, 2)
        quant(2, 2, 4)
        mm(1)
        finish(0)
        mm(2)
        finish(1)
        permute(4)

        for tick in range(4, NG - 1):
            transposes(tick, False)
            new_codes(tick - 1)
            quant(tick - 1, 0, 2)
            quant(tick - 1, 2, 4)
            mm(tick - 1)
            finish(tick - 2)
            permute(tick + 1)

        last = NG - 1
        transposes(last, False)
        new_codes(last - 1)
        quant(last - 1, 0, 2)
        quant(last - 1, 2, 4)
        new_codes(last)
        quant(last, 0, 1)
        finish(last - 2)
        quant(last, 1, 2)
        quant(last, 2, 3)
        quant(last, 3, 4)
        mm(last - 1)
        mm(last)
        finish(last - 1)
        finish(last)
